import numpy as np
import ml_dtypes


def mxq(x, axis, fmt="e4m3"):
    dtype, down = {"e4m3": (ml_dtypes.float8_e4m3fn, 7), "e5m2": (ml_dtypes.float8_e5m2, 14)}[fmt]
    v = np.moveaxis(np.asarray(x, np.float32).astype(ml_dtypes.bfloat16).astype(np.float64), axis, -1)
    blocks = v.reshape(v.shape[:-1] + (-1, 32))
    amax = np.abs(blocks).max(-1, keepdims=True)
    byte = np.maximum(np.where(amax > 0, np.frexp(amax)[1] - 1 + 127, 0) - down, 1)
    scale = np.exp2(byte - 127.0)
    codes = (blocks / scale).astype(np.float32).astype(dtype).astype(np.float64)
    return np.moveaxis((codes * scale).reshape(v.shape), -1, axis)


WIDE = False


def mx_kscale(k):
    if not WIDE:
        return np.ones(k)
    levels = np.array([10, -10, 5, -5, 0])
    a = np.random.permutation(np.resize(levels, k // 512 * 4)).reshape(k // 512, 4)
    idx = np.arange(k)
    return np.exp2(a[idx // 512, idx % 128 // 32])


BF16 = ml_dtypes.bfloat16


def bf(x):
    return np.asarray(x, np.float32).astype(BF16)


def f64(x):
    return np.asarray(x).astype(np.float64)


B, T, N, C = 2, 2, 512, 1024
EDGE = 0.0625


def sigmoid(z):
    return 1.0 / (1.0 + np.exp(-z))


def setup_inputs():
    s = mx_kscale(C)
    return {"x": bf(np.random.standard_normal((B, T, N, C)) * 0.5),
            "hid": bf(np.maximum(np.random.standard_normal((B, T, N, C)), 0.0) * s),
            "adj": bf(np.random.random((B, N, N)) * (np.random.random((B, N, N)) < EDGE)),
            "lam_raw": bf(3.5 + 0.1 * np.random.standard_normal(1)),
            "theta": bf(np.random.standard_normal((C, C)) * 4.5 / np.sqrt(C) / s[:, None])}


def reference(x, hid, adj, lam_raw, theta):
    lam = 1.0 + np.maximum(f64(lam_raw)[0], 0.0)
    h = mxq(f64(hid), 3, "e4m3") @ mxq(f64(theta), 0, "e4m3")
    v = ((2.0 * lam - 2.0) / lam) * np.eye(N) + (2.0 / lam) * f64(adj)
    v = v / np.sum(v, axis=-1, keepdims=True)
    out = mxq(v, 2, "e4m3")[:, None] @ mxq(h, 2, "e4m3")
    return np.maximum(f64(x), 0.0) + sigmoid(np.maximum(out, 0.0))

@@ -1,0 +1,397 @@
+from contextlib import ExitStack
+
+import concourse.mybir as mybir
+from concourse.masks import make_identity
+
+F32 = mybir.dt.float32
+BF16 = mybir.dt.bfloat16
+U32 = mybir.dt.uint32
+U8 = mybir.dt.uint8
+FP8X4 = mybir.dt.float8_e4m3fn_x4
+ALU = mybir.AluOpType
+ACT = mybir.ActivationFunctionType
+AX = mybir.AxisListType
+
+P = 128
+B, T, N, C = 2, 2, 512, 1024
+FLOPS = 2 * B * T * N * C * C + 2 * B * T * N * N * C
+PINNED = True
+
+
+def tile_akgcn_pb_kernel(tc, x, hid, adj, lam_raw, theta, out):
+    nc = tc.nc
+    with ExitStack() as ctx:
+        if PINNED:
+            ctx.enter_context(tc.manual_schedule())
+        const = ctx.enter_context(tc.tile_pool(name="const", bufs=1))
+        res = ctx.enter_context(tc.tile_pool(name="res", bufs=1))
+        two = ctx.enter_context(tc.tile_pool(name="two", bufs=2))
+        three = ctx.enter_context(tc.tile_pool(name="three", bufs=3))
+        four = ctx.enter_context(tc.tile_pool(name="four", bufs=4))
+        ps_t = ctx.enter_context(tc.psum_pool(name="ps_t", bufs=4))
+        ps_h = ctx.enter_context(tc.psum_pool(name="ps_h", bufs=2))
+        ps_o = ctx.enter_context(tc.psum_pool(name="ps_o", bufs=2))
+
+        def eng(e):
+            return nc.vector if e == "V" else nc.scalar
+
+        def copy(e, dst, src):
+            if e == "V":
+                nc.vector.tensor_copy(out=dst, in_=src)
+            else:
+                nc.scalar.copy(out=dst, in_=src)
+
+        ident_f = const.tile([P, P], F32)
+        make_identity(nc, ident_f[:])
+        ident_b = const.tile([P, P], BF16)
+        make_identity(nc, ident_b[:])
+        warm = const.tile([P, 1], F32)
+        nc.vector.memset(warm[:], 0.0)
+        warm2 = const.tile([P, 1], F32)
+        nc.scalar.activation(out=warm2[:], in_=warm[:], func=ACT.Sigmoid)
+
+        lam_b = const.tile([P, 1], BF16)
+        nc.scalar.dma_start(out=lam_b[:], in_=lam_raw.partition_broadcast(P))
+
+        adj_sb = []
+        for b in range(B):
+            a_t = res.tile([P, 4 * N], BF16, name="adj%d" % b)
+            adj_sb.append(a_t)
+        hid_sb = []
+        x_sb = []
+        for bt in range(B * T):
+            h_t = res.tile([P, 4 * C], BF16, name="hid%d" % bt)
+            hid_sb.append(h_t)
+            x_t = res.tile([P, 4 * C], BF16, name="x%d" % bt)
+            x_sb.append(x_t)
+        th_raw = []
+        for ch in range(2):
+            t_t = res.tile([P, 8 * 512], BF16, name="thraw%d" % ch)
+            th_raw.append(t_t)
+
+        def load_adj(b):
+            nc.sync.dma_start(out=adj_sb[b][:], in_=adj[b].rearrange("(p j) m -> p (j m)", j=4))
+
+        def load_hid(bt):
+            nc.sync.dma_start(
+                out=hid_sb[bt][:], in_=hid[bt // T, bt % T].rearrange("(p j) c -> p (j c)", j=4)
+            )
+
+        def load_x(bt):
+            nc.sync.dma_start(
+                out=x_sb[bt][:], in_=x[bt // T, bt % T].rearrange("(p j) c -> p (j c)", j=4)
+            )
+
+        def load_theta(ch):
+            for a in range(4):
+                nc.sync.dma_start(
+                    out=th_raw[ch][:, a * 1024 : (a + 1) * 1024].rearrange("q (e c) -> q e c", e=2),
+                    in_=theta[a * 256 : (a + 1) * 256, ch * 512 : (ch + 1) * 512].rearrange(
+                        "(q e) c -> q e c", e=2
+                    ),
+                )
+
+        load_adj(0)
+        load_adj(1)
+        load_hid(0)
+        load_theta(0)
+        load_theta(1)
+        load_hid(1)
+        load_x(0)
+        load_hid(2)
+        load_x(1)
+        load_hid(3)
+        load_x(2)
+        load_x(3)
+
+        g32 = const.tile([P, 1], F32)
+        nc.vector.tensor_scalar_max(out=g32[:], in0=lam_b[:], scalar1=0.0)
+
+        th_q = res.tile([P, 2048], U32, align_bytes=64)
+        th_s = res.tile([P, 2048], U8, align_bytes=64)
+        v_q = []
+        v_s = []
+        for b in range(B):
+            q_t = res.tile([P, 512], U32, name="vq%d" % b, align_bytes=64)
+            s_t = res.tile([P, 512], U8, name="vs%d" % b, align_bytes=64)
+            v_q.append(q_t)
+            v_s.append(s_t)
+
+        st = {}
+
+        def V1(b, e):
+            rs = two.tile([P, 4], F32, name="rs")
+            st["rs", b] = rs
+            if e == "V":
+                nc.vector.tensor_reduce(
+                    out=rs[:], in_=adj_sb[b][:].rearrange("p (j m) -> p j m", j=4), axis=AX.X, op=ALU.add
+                )
+            else:
+                for j in range(4):
+                    junk = const.tile([P, N], BF16, name="junk")
+                    nc.scalar.activation(
+                        out=junk[:],
+                        in_=adj_sb[b][:, j * N : (j + 1) * N],
+                        func=ACT.Copy,
+                        accum_out=rs[:, j : j + 1],
+                    )
+
+        def Vs(b):
+            den = two.tile([P, 4], F32, name="den")
+            nc.vector.tensor_scalar(
+                out=den[:], in0=st["rs", b][:], scalar1=g32[:, 0:1], scalar2=None, op0=ALU.add
+            )
+            rec = two.tile([P, 4], F32, name="rec")
+            nc.vector.reciprocal(out=rec[:], in_=den[:])
+            grec = two.tile([P, 4], F32, name="grec")
+            nc.vector.tensor_scalar(
+                out=grec[:], in0=rec[:], scalar1=g32[:, 0:1], scalar2=None, op0=ALU.mult
+            )
+            st["rec", b] = rec
+            st["grec", b] = grec
+            vperm = const.tile([P, 4 * N], BF16, name="vperm")
+            st["vperm", b] = vperm
+
+        def V2(b, j):
+            src = adj_sb[b][:, j * N : (j + 1) * N].rearrange("q (p t) -> q t p", t=4)
+            nc.vector.tensor_scalar(
+                out=st["vperm", b][:, j * N : (j + 1) * N].rearrange("q (t p) -> q t p", t=4),
+                in0=src,
+                scalar1=st["rec", b][:, j : j + 1],
+                scalar2=None,
+                op0=ALU.mult,
+            )
+
+        def VD(b, j):
+            src = adj_sb[b][:, j * N : (j + 1) * N].rearrange("q (p t) -> q t p", t=4)
+            dg = two.tile([P, P], F32, name="dg")
+            nc.vector.tensor_scalar(
+                out=dg[:], in0=ident_f[:], scalar1=st["grec", b][:, j : j + 1], scalar2=None, op0=ALU.mult
+            )
+            nc.vector.scalar_tensor_tensor(
+                out=st["vperm", b][:, j * N + j * P : j * N + (j + 1) * P],
+                in0=src[:, j, :],
+                scalar=st["rec", b][:, j : j + 1],
+                in1=dg[:],
+                op0=ALU.mult,
+                op1=ALU.add,
+            )
+
+        def TV(b, jp):
+            vt = ps_t.tile([P, 1024], BF16, tag="tp", name="vt")
+            st["vt", b, jp] = vt
+            for i in range(8):
+                nc.tensor.transpose(
+                    vt[:, i * P : (i + 1) * P],
+                    st["vperm", b][:, (jp * 8 + i) * P : (jp * 8 + i + 1) * P],
+                    ident_b[:],
+                )
+
+        def EV(b, jp, e):
+            if jp == 0:
+                vgrp = const.tile([P, 4 * N], BF16, name="vgrp", align_bytes=64)
+                st["vgrp", b] = vgrp
+            copy(
+                e,
+                st["vgrp", b][:, jp * 1024 : (jp + 1) * 1024].rearrange("p (j n t) -> p j n t", j=2, t=4),
+                st["vt", b, jp][:].rearrange("p (j t n) -> p j n t", j=2, t=4),
+            )
+
+        def QV(b):
+            nc.vector.quantize_mx(out=v_q[b][:].bitcast(FP8X4), scales=v_s[b][:], in_=st["vgrp", b][:])
+
+        def RT(ch, g, e):
+            if g == 0:
+                tg = two.tile([P, 4096], BF16, name="tg", align_bytes=64)
+                st["tg", ch] = tg
+            copy(
+                e,
+                st["tg", ch][:, g * 2048 : (g + 1) * 2048].rearrange("p (c i t) -> p c t i", i=4, t=4),
+                th_raw[ch][:, g * 2048 : (g + 1) * 2048].rearrange("p (t c i) -> p c t i", t=4, i=4),
+            )
+
+        def QT(ch):
+            nc.vector.quantize_mx(
+                out=th_q[:, ch * 1024 : (ch + 1) * 1024].bitcast(FP8X4),
+                scales=th_s[:, ch * 1024 : (ch + 1) * 1024],
+                in_=st["tg", ch][:],
+            )
+
+        def TA(bt, j):
+            hw = hid_sb[bt][:].bitcast(F32)
+            xt = ps_t.tile([P, 512], F32, tag="tp", name="xt")
+            st["xt", bt, j] = xt
+            for a in range(4):
+                nc.tensor.transpose(
+                    xt[:, a * P : (a + 1) * P],
+                    hw[:, j * 512 + a * P : j * 512 + (a + 1) * P],
+                    ident_f[:],
+                )
+
+        def EA(bt, j, e):
+            if j == 0:
+                hg = two.tile([P, 4096], BF16, name="hg", align_bytes=64)
+                st["hg", bt] = hg
+            hgw = st["hg", bt][:].bitcast(F32)
+            copy(
+                e,
+                hgw[:, j * 512 : (j + 1) * 512].rearrange("p (g r u) -> p g r u", g=2, u=2),
+                st["xt", bt, j][:].rearrange("p (g u r) -> p g r u", g=2, u=2),
+            )
+
+        def QA(bt, h):
+            if h == 0:
+                hq = three.tile([P, 1024], U32, name="hq", align_bytes=64)
+                hs = three.tile([P, 1024], U8, name="hs", align_bytes=64)
+                st["hq", bt] = (hq, hs)
+            hq, hs = st["hq", bt]
+            nc.vector.quantize_mx(
+                out=hq[:, h * 512 : (h + 1) * 512].bitcast(FP8X4),
+                scales=hs[:, h * 512 : (h + 1) * 512],
+                in_=st["hg", bt][:, h * 2048 : (h + 1) * 2048],
+            )
+
+        def A(bt, n_scalar):
+            for j in range(4):
+                TA(bt, j)
+            for j in range(4):
+                EA(bt, j, "S" if j < n_scalar else "V")
+                if j % 2 == 1:
+                    QA(bt, j // 2)
+
+        def M1(u, k):
+            bt, ch = u // 2, u % 2
+            hq, hs = st["hq", bt]
+            hp = ps_h.tile([P, 512], F32, tag="hp", name="hp")
+            st["hp", u, k] = hp
+            for j in range(4):
+                for g in range(2):
+                    lo = (j * 2 + g) * P
+                    ro = ch * 1024 + g * 512 + k * P
+                    nc.tensor.matmul_mx(
+                        out=hp[:, j * P : (j + 1) * P],
+                        lhsT=hq[:, lo : lo + P].bitcast(FP8X4),
+                        lhsT_scale=hs[:, lo : lo + P],
+                        rhs=th_q[:, ro : ro + P].bitcast(FP8X4),
+                        rhs_scale=th_s[:, ro : ro + P],
+                        start=(g == 0),
+                        stop=(g == 1),
+                    )
+
+        def EH(u, k, e):
+            if k == 0:
+                h2g = four.tile([P, 2048], BF16, name="h2g", align_bytes=64)
+                st["h2g", u] = h2g
+            copy(
+                e,
+                st["h2g", u][:, k * 512 : (k + 1) * 512].rearrange("p (c j) -> p c j", j=4),
+                st["hp", u, k][:].rearrange("p (j c) -> p c j", j=4),
+            )
+
+        def QH(u):
+            h2q = four.tile([P, 512], U32, name="h2q", align_bytes=64)
+            h2s = four.tile([P, 512], U8, name="h2s", align_bytes=64)
+            st["h2q", u] = (h2q, h2s)
+            nc.vector.quantize_mx(out=h2q[:].bitcast(FP8X4), scales=h2s[:], in_=st["h2g", u][:])
+
+        def xview(u):
+            bt, ch = u // 2, u % 2
+            return x_sb[bt][:].rearrange("p (j c) -> p j c", j=4)[:, :, ch * 512 : (ch + 1) * 512]
+
+        def RX(u):
+            nc.vector.tensor_scalar_max(out=xview(u), in0=xview(u), scalar1=0.0)
+
+        def M2(u, jn):
+            b = u // 4
+            h2q, h2s = st["h2q", u]
+            op = ps_o.tile([P, 512], F32, tag="op", name="op")
+            st["op", u, jn] = op
+            nc.tensor.matmul_mx(
+                out=op[:],
+                lhsT=v_q[b][:, jn * P : (jn + 1) * P].bitcast(FP8X4),
+                lhsT_scale=v_s[b][:, jn * P : (jn + 1) * P],
+                rhs=h2q[:].bitcast(FP8X4),
+                rhs_scale=h2s[:],
+                start=True,
+                stop=True,
+            )
+
+        def SG(u, jn):
+            if jn == 0:
+                ot = four.tile([P, 2048], F32, name="ot")
+                st["ot", u] = ot
+            nc.scalar.activation(
+                out=st["ot", u][:, jn * 512 : (jn + 1) * 512], in_=st["op", u, jn][:], func=ACT.Sigmoid
+            )
+
+        def ST(u, j0, j1):
+            bt, ch = u // 2, u % 2
+            o3 = st["ot", u][:].rearrange("p (j c) -> p j c", j=4)[:, j0:j1, :]
+            nc.vector.scalar_tensor_tensor(
+                out=o3, in0=o3, scalar=0.5, in1=xview(u)[:, j0:j1, :], op0=ALU.max, op1=ALU.add
+            )
+            o_v = out[bt // T, bt % T].rearrange("(p j) c -> p j c", j=4)
+            nc.sync.dma_start(out=o_v[:, j0:j1, ch * 512 : (ch + 1) * 512], in_=o3)
+
+        V1(0, "V")
+        V1(1, "S")
+        Vs(0)
+        for j in range(4):
+            V2(0, j)
+        for j in range(4):
+            VD(0, j)
+        for j in range(4):
+            TA(0, j)
+        for j in range(4):
+            EA(0, j, "S")
+        TV(0, 0)
+        TV(0, 1)
+        EV(0, 0, "V")
+        EV(0, 1, "S")
+        QA(0, 0)
+        QV(0)
+        RT(0, 0, "V")
+        RT(0, 1, "S")
+        QA(0, 1)
+        RT(1, 0, "V")
+        RT(1, 1, "S")
+        QT(0)
+        QT(1)
+        A(1, 2)
+
+        for u in range(10):
+            w, z = u - 1, u - 2
+            if u == 2:
+                TV(1, 0)
+                TV(1, 1)
+                EV(1, 0, "V")
+                EV(1, 1, "V")
+                QV(1)
+            if u < 8:
+                M1(u, 0)
+                M1(u, 1)
+            if 0 <= z < 7:
+                ST(z, 0, 4)
+            if z == 7:
+                for j in range(4):
+                    ST(z, j, j + 1)
+            for k in range(4):
+                if u < 8:
+                    if k >= 2:
+                        M1(u, k)
+                    EH(u, k, "V" if (k == 3 and u != 2) else "S")
+                if 0 <= w < 8:
+                    M2(w, k)
+                    SG(w, k)
+            if u < 8:
+                QH(u)
+                RX(u)
+            if u == 0:
+                Vs(1)
+                for j in range(4):
+                    V2(1, j)
+                for j in range(4):
+                    VD(1, j)
+                A(2, 4)
+            if u == 2:
+                A(3, 4)

@@ -28,9 +28,7 @@ def tile_akgcn_pb_kernel(tc, x, hid, adj, lam_raw, theta, out):
         two = ctx.enter_context(tc.tile_pool(name="two", bufs=2))
         three = ctx.enter_context(tc.tile_pool(name="three", bufs=3))
         four = ctx.enter_context(tc.tile_pool(name="four", bufs=4))
-        ps_t = ctx.enter_context(tc.psum_pool(name="ps_t", bufs=4))
-        ps_h = ctx.enter_context(tc.psum_pool(name="ps_h", bufs=2))
-        ps_o = ctx.enter_context(tc.psum_pool(name="ps_o", bufs=2))
+        ps = ctx.enter_context(tc.psum_pool(name="ps", bufs=8))
 
         def eng(e):
             return nc.vector if e == "V" else nc.scalar
@@ -51,7 +49,7 @@ def tile_akgcn_pb_kernel(tc, x, hid, adj, lam_raw, theta, out):
         nc.scalar.activation(out=warm2[:], in_=warm[:], func=ACT.Sigmoid)
 
         lam_b = const.tile([P, 1], BF16)
-        nc.scalar.dma_start(out=lam_b[:], in_=lam_raw.partition_broadcast(P))
+        nc.sync.dma_start(out=lam_b[:], in_=lam_raw.partition_broadcast(P))
 
         adj_sb = []
         for b in range(B):
@@ -97,15 +95,14 @@ def tile_akgcn_pb_kernel(tc, x, hid, adj, lam_raw, theta, out):
         load_theta(0)
         load_theta(1)
         load_hid(1)
-        load_x(0)
         load_hid(2)
-        load_x(1)
+        load_x(0)
         load_hid(3)
+        load_x(1)
         load_x(2)
         load_x(3)
 
         g32 = const.tile([P, 1], F32)
-        nc.vector.tensor_scalar_max(out=g32[:], in0=lam_b[:], scalar1=0.0)
 
         th_q = res.tile([P, 2048], U32, align_bytes=64)
         th_s = res.tile([P, 2048], U8, align_bytes=64)
@@ -178,7 +175,7 @@ def tile_akgcn_pb_kernel(tc, x, hid, adj, lam_raw, theta, out):
             )
 
         def TV(b, jp):
-            vt = ps_t.tile([P, 1024], BF16, tag="tp", name="vt")
+            vt = ps.tile([P, 1024], BF16, tag="ps", name="vt")
             st["vt", b, jp] = vt
             for i in range(8):
                 nc.tensor.transpose(
@@ -219,7 +216,7 @@ def tile_akgcn_pb_kernel(tc, x, hid, adj, lam_raw, theta, out):
 
         def TA(bt, j):
             hw = hid_sb[bt][:].bitcast(F32)
-            xt = ps_t.tile([P, 512], F32, tag="tp", name="xt")
+            xt = ps.tile([P, 512], F32, tag="ps", name="xt")
             st["xt", bt, j] = xt
             for a in range(4):
                 nc.tensor.transpose(
@@ -262,7 +259,7 @@ def tile_akgcn_pb_kernel(tc, x, hid, adj, lam_raw, theta, out):
         def M1(u, k):
             bt, ch = u // 2, u % 2
             hq, hs = st["hq", bt]
-            hp = ps_h.tile([P, 512], F32, tag="hp", name="hp")
+            hp = ps.tile([P, 512], F32, tag="ps", name="hp")
             st["hp", u, k] = hp
             for j in range(4):
                 for g in range(2):
@@ -280,7 +277,7 @@ def tile_akgcn_pb_kernel(tc, x, hid, adj, lam_raw, theta, out):
 
         def EH(u, k, e):
             if k == 0:
-                h2g = four.tile([P, 2048], BF16, name="h2g", align_bytes=64)
+                h2g = three.tile([P, 2048], BF16, name="h2g", align_bytes=64)
                 st["h2g", u] = h2g
             copy(
                 e,
@@ -304,7 +301,7 @@ def tile_akgcn_pb_kernel(tc, x, hid, adj, lam_raw, theta, out):
         def M2(u, jn):
             b = u // 4
             h2q, h2s = st["h2q", u]
-            op = ps_o.tile([P, 512], F32, tag="op", name="op")
+            op = ps.tile([P, 512], F32, tag="ps", name="op")
             st["op", u, jn] = op
             nc.tensor.matmul_mx(
                 out=op[:],
@@ -335,6 +332,7 @@ def tile_akgcn_pb_kernel(tc, x, hid, adj, lam_raw, theta, out):
 
         V1(0, "V")
         V1(1, "S")
+        nc.vector.tensor_scalar_max(out=g32[:], in0=lam_b[:], scalar1=0.0)
         Vs(0)
         for j in range(4):
             V2(0, j)
@@ -357,16 +355,20 @@ def tile_akgcn_pb_kernel(tc, x, hid, adj, lam_raw, theta, out):
         RT(1, 1, "S")
         QT(0)
         QT(1)
-        A(1, 2)
 
-        for u in range(10):
-            w, z = u - 1, u - 2
+        for u in range(11):
+            w, z = u - 2, u - 3
+            if u == 0:
+                A(1, 4)
+                Vs(1)
+                for j in range(4):
+                    V2(1, j)
+                for j in range(4):
+                    VD(1, j)
+            if u == 1:
+                A(2, 4)
             if u == 2:
-                TV(1, 0)
-                TV(1, 1)
-                EV(1, 0, "V")
-                EV(1, 1, "V")
-                QV(1)
+                A(3, 3)
             if u < 8:
                 M1(u, 0)
                 M1(u, 1)
@@ -379,19 +381,17 @@ def tile_akgcn_pb_kernel(tc, x, hid, adj, lam_raw, theta, out):
                 if u < 8:
                     if k >= 2:
                         M1(u, k)
-                    EH(u, k, "V" if (k == 3 and u != 2) else "S")
+                    EH(u, k, "V" if (k == 3 and u != 0) else "S")
                 if 0 <= w < 8:
                     M2(w, k)
                     SG(w, k)
             if u < 8:
                 QH(u)
-                RX(u)
-            if u == 0:
-                Vs(1)
-                for j in range(4):
-                    V2(1, j)
-                for j in range(4):
-                    VD(1, j)
-                A(2, 4)
-            if u == 2:
-                A(3, 4)
+            if 1 <= u <= 8:
+                RX(u - 1)
+            if u == 1:
+                TV(1, 0)
+                TV(1, 1)
+                EV(1, 0, "S")
+                EV(1, 1, "V")
+                QV(1)

@@ -15,7 +15,7 @@ AX = mybir.AxisListType
 P = 128
 B, T, N, C = 2, 2, 512, 1024
 FLOPS = 2 * B * T * N * C * C + 2 * B * T * N * N * C
-PINNED = True
+PINNED = False
 
 
 def tile_akgcn_pb_kernel(tc, x, hid, adj, lam_raw, theta, out):

@@ -133,6 +133,14 @@ def tile_akgcn_pb_kernel(tc, x, hid, adj, lam_raw, theta, out):
                         accum_out=rs[:, j : j + 1],
                     )
 
+        g_diag = const.tile([P, P], BF16)
+
+        def G():
+            nc.vector.tensor_scalar_max(out=g32[:], in0=lam_b[:], scalar1=0.0)
+            nc.vector.tensor_scalar(
+                out=g_diag[:], in0=ident_b[:], scalar1=g32[:, 0:1], scalar2=None, op0=ALU.mult
+            )
+
         def Vs(b):
             den = two.tile([P, 4], F32, name="den")
             nc.vector.tensor_scalar(
@@ -140,58 +148,44 @@ def tile_akgcn_pb_kernel(tc, x, hid, adj, lam_raw, theta, out):
             )
             rec = two.tile([P, 4], F32, name="rec")
             nc.vector.reciprocal(out=rec[:], in_=den[:])
-            grec = two.tile([P, 4], F32, name="grec")
-            nc.vector.tensor_scalar(
-                out=grec[:], in0=rec[:], scalar1=g32[:, 0:1], scalar2=None, op0=ALU.mult
-            )
             st["rec", b] = rec
-            st["grec", b] = grec
-            vperm = const.tile([P, 4 * N], BF16, name="vperm")
-            st["vperm", b] = vperm
 
-        def V2(b, j):
+        def VW(b, j):
+            wp = ps.tile([P, 512], F32, tag="ps", name="wp")
+            st["wp", b, j] = wp
             src = adj_sb[b][:, j * N : (j + 1) * N].rearrange("q (p t) -> q t p", t=4)
-            nc.vector.tensor_scalar(
-                out=st["vperm", b][:, j * N : (j + 1) * N].rearrange("q (t p) -> q t p", t=4),
-                in0=src,
-                scalar1=st["rec", b][:, j : j + 1],
-                scalar2=None,
-                op0=ALU.mult,
-            )
-
-        def VD(b, j):
-            src = adj_sb[b][:, j * N : (j + 1) * N].rearrange("q (p t) -> q t p", t=4)
-            dg = two.tile([P, P], F32, name="dg")
-            nc.vector.tensor_scalar(
-                out=dg[:], in0=ident_f[:], scalar1=st["grec", b][:, j : j + 1], scalar2=None, op0=ALU.mult
-            )
-            nc.vector.scalar_tensor_tensor(
-                out=st["vperm", b][:, j * N + j * P : j * N + (j + 1) * P],
-                in0=src[:, j, :],
-                scalar=st["rec", b][:, j : j + 1],
-                in1=dg[:],
-                op0=ALU.mult,
-                op1=ALU.add,
-            )
-
-        def TV(b, jp):
-            vt = ps.tile([P, 1024], BF16, tag="ps", name="vt")
-            st["vt", b, jp] = vt
-            for i in range(8):
-                nc.tensor.transpose(
-                    vt[:, i * P : (i + 1) * P],
-                    st["vperm", b][:, (jp * 8 + i) * P : (jp * 8 + i + 1) * P],
-                    ident_b[:],
+            for t in range(4):
+                nc.tensor.matmul(
+                    out=wp[:, t * P : (t + 1) * P], lhsT=src[:, t, :], rhs=ident_b[:], start=True, stop=(t != j)
                 )
+                if t == j:
+                    nc.tensor.matmul(
+                        out=wp[:, t * P : (t + 1) * P], lhsT=ident_b[:], rhs=g_diag[:], start=False, stop=True
+                    )
 
-        def EV(b, jp, e):
-            if jp == 0:
+        def VR(b):
+            rp = ps.tile([P, 512], F32, tag="ps", name="rp")
+            for j in range(4):
+                nc.tensor.matmul(
+                    out=rp[:, j * P : (j + 1) * P],
+                    lhsT=st["rec", b][:, j : j + 1].to_broadcast([P, P]),
+                    rhs=ident_f[:],
+                    start=True,
+                    stop=True,
+                )
+            rsb = two.tile([P, 512], F32, name="rsb")
+            st["rsb", b] = rsb
+            nc.scalar.copy(out=rsb[:], in_=rp[:])
+
+        def VM(b, j):
+            if j == 0:
                 vgrp = const.tile([P, 4 * N], BF16, name="vgrp", align_bytes=64)
                 st["vgrp", b] = vgrp
-            copy(
-                e,
-                st["vgrp", b][:, jp * 1024 : (jp + 1) * 1024].rearrange("p (j n t) -> p j n t", j=2, t=4),
-                st["vt", b, jp][:].rearrange("p (j t n) -> p j n t", j=2, t=4),
+            nc.vector.tensor_tensor(
+                out=st["vgrp", b][:, j * N : (j + 1) * N].rearrange("p (n t) -> p n t", t=4),
+                in0=st["wp", b, j][:].rearrange("p (t n) -> p n t", t=4),
+                in1=st["rsb", b][:, j * P : (j + 1) * P].unsqueeze(2).to_broadcast([P, P, 4]),
+                op=ALU.mult,
             )
 
         def QV(b):
@@ -332,20 +326,17 @@ def tile_akgcn_pb_kernel(tc, x, hid, adj, lam_raw, theta, out):
 
         V1(0, "V")
         V1(1, "S")
-        nc.vector.tensor_scalar_max(out=g32[:], in0=lam_b[:], scalar1=0.0)
+        G()
+        for j in range(4):
+            VW(0, j)
         Vs(0)
-        for j in range(4):
-            V2(0, j)
-        for j in range(4):
-            VD(0, j)
+        VR(0)
         for j in range(4):
             TA(0, j)
         for j in range(4):
             EA(0, j, "S")
-        TV(0, 0)
-        TV(0, 1)
-        EV(0, 0, "V")
-        EV(0, 1, "S")
+        for j in range(4):
+            VM(0, j)
         QA(0, 0)
         QV(0)
         RT(0, 0, "V")
@@ -361,10 +352,7 @@ def tile_akgcn_pb_kernel(tc, x, hid, adj, lam_raw, theta, out):
             if u == 0:
                 A(1, 4)
                 Vs(1)
-                for j in range(4):
-                    V2(1, j)
-                for j in range(4):
-                    VD(1, j)
+                VR(1)
             if u == 1:
                 A(2, 4)
             if u == 2:
@@ -381,7 +369,7 @@ def tile_akgcn_pb_kernel(tc, x, hid, adj, lam_raw, theta, out):
                 if u < 8:
                     if k >= 2:
                         M1(u, k)
-                    EH(u, k, "V" if (k == 3 and u != 0) else "S")
+                    EH(u, k, "V" if k == 3 else "S")
                 if 0 <= w < 8:
                     M2(w, k)
                     SG(w, k)
@@ -390,8 +378,8 @@ def tile_akgcn_pb_kernel(tc, x, hid, adj, lam_raw, theta, out):
             if 1 <= u <= 8:
                 RX(u - 1)
             if u == 1:
-                TV(1, 0)
-                TV(1, 1)
-                EV(1, 0, "S")
-                EV(1, 1, "V")
+                for j in range(4):
+                    VW(1, j)
+                for j in range(4):
+                    VM(1, j)
                 QV(1)

@@ -16,6 +16,7 @@ P = 128
 B, T, N, C = 2, 2, 512, 1024
 FLOPS = 2 * B * T * N * C * C + 2 * B * T * N * N * C
 PINNED = False
+ST_PIECES = (4, 4, 4, 4, 4, 4, 4, 4)
 
 
 def tile_akgcn_pb_kernel(tc, x, hid, adj, lam_raw, theta, out):
@@ -133,14 +134,6 @@ def tile_akgcn_pb_kernel(tc, x, hid, adj, lam_raw, theta, out):
                         accum_out=rs[:, j : j + 1],
                     )
 
-        g_diag = const.tile([P, P], BF16)
-
-        def G():
-            nc.vector.tensor_scalar_max(out=g32[:], in0=lam_b[:], scalar1=0.0)
-            nc.vector.tensor_scalar(
-                out=g_diag[:], in0=ident_b[:], scalar1=g32[:, 0:1], scalar2=None, op0=ALU.mult
-            )
-
         def Vs(b):
             den = two.tile([P, 4], F32, name="den")
             nc.vector.tensor_scalar(
@@ -148,44 +141,58 @@ def tile_akgcn_pb_kernel(tc, x, hid, adj, lam_raw, theta, out):
             )
             rec = two.tile([P, 4], F32, name="rec")
             nc.vector.reciprocal(out=rec[:], in_=den[:])
+            grec = two.tile([P, 4], F32, name="grec")
+            nc.vector.tensor_scalar(
+                out=grec[:], in0=rec[:], scalar1=g32[:, 0:1], scalar2=None, op0=ALU.mult
+            )
             st["rec", b] = rec
+            st["grec", b] = grec
+            vperm = const.tile([P, 4 * N], BF16, name="vperm")
+            st["vperm", b] = vperm
 
-        def VW(b, j):
-            wp = ps.tile([P, 512], F32, tag="ps", name="wp")
-            st["wp", b, j] = wp
+        def V2(b, j):
             src = adj_sb[b][:, j * N : (j + 1) * N].rearrange("q (p t) -> q t p", t=4)
-            for t in range(4):
-                nc.tensor.matmul(
-                    out=wp[:, t * P : (t + 1) * P], lhsT=src[:, t, :], rhs=ident_b[:], start=True, stop=(t != j)
-                )
-                if t == j:
-                    nc.tensor.matmul(
-                        out=wp[:, t * P : (t + 1) * P], lhsT=ident_b[:], rhs=g_diag[:], start=False, stop=True
-                    )
+            nc.vector.tensor_scalar(
+                out=st["vperm", b][:, j * N : (j + 1) * N].rearrange("q (t p) -> q t p", t=4),
+                in0=src,
+                scalar1=st["rec", b][:, j : j + 1],
+                scalar2=None,
+                op0=ALU.mult,
+            )
 
-        def VR(b):
-            rp = ps.tile([P, 512], F32, tag="ps", name="rp")
-            for j in range(4):
-                nc.tensor.matmul(
-                    out=rp[:, j * P : (j + 1) * P],
-                    lhsT=st["rec", b][:, j : j + 1].to_broadcast([P, P]),
-                    rhs=ident_f[:],
-                    start=True,
-                    stop=True,
-                )
-            rsb = two.tile([P, 512], F32, name="rsb")
-            st["rsb", b] = rsb
-            nc.scalar.copy(out=rsb[:], in_=rp[:])
+        def VD(b, j):
+            src = adj_sb[b][:, j * N : (j + 1) * N].rearrange("q (p t) -> q t p", t=4)
+            dg = two.tile([P, P], F32, name="dg")
+            nc.vector.tensor_scalar(
+                out=dg[:], in0=ident_f[:], scalar1=st["grec", b][:, j : j + 1], scalar2=None, op0=ALU.mult
+            )
+            nc.vector.scalar_tensor_tensor(
+                out=st["vperm", b][:, j * N + j * P : j * N + (j + 1) * P],
+                in0=src[:, j, :],
+                scalar=st["rec", b][:, j : j + 1],
+                in1=dg[:],
+                op0=ALU.mult,
+                op1=ALU.add,
+            )
 
-        def VM(b, j):
-            if j == 0:
+        def TV(b, jp):
+            vt = ps.tile([P, 1024], BF16, tag="ps", name="vt")
+            st["vt", b, jp] = vt
+            for i in range(8):
+                nc.tensor.transpose(
+                    vt[:, i * P : (i + 1) * P],
+                    st["vperm", b][:, (jp * 8 + i) * P : (jp * 8 + i + 1) * P],
+                    ident_b[:],
+                )
+
+        def EV(b, jp, e):
+            if jp == 0:
                 vgrp = const.tile([P, 4 * N], BF16, name="vgrp", align_bytes=64)
                 st["vgrp", b] = vgrp
-            nc.vector.tensor_tensor(
-                out=st["vgrp", b][:, j * N : (j + 1) * N].rearrange("p (n t) -> p n t", t=4),
-                in0=st["wp", b, j][:].rearrange("p (t n) -> p n t", t=4),
-                in1=st["rsb", b][:, j * P : (j + 1) * P].unsqueeze(2).to_broadcast([P, P, 4]),
-                op=ALU.mult,
+            copy(
+                e,
+                st["vgrp", b][:, jp * 1024 : (jp + 1) * 1024].rearrange("p (j n t) -> p j n t", j=2, t=4),
+                st["vt", b, jp][:].rearrange("p (j t n) -> p j n t", j=2, t=4),
             )
 
         def QV(b):
@@ -326,17 +333,20 @@ def tile_akgcn_pb_kernel(tc, x, hid, adj, lam_raw, theta, out):
 
         V1(0, "V")
         V1(1, "S")
-        G()
-        for j in range(4):
-            VW(0, j)
+        nc.vector.tensor_scalar_max(out=g32[:], in0=lam_b[:], scalar1=0.0)
         Vs(0)
-        VR(0)
+        for j in range(4):
+            V2(0, j)
+        for j in range(4):
+            VD(0, j)
         for j in range(4):
             TA(0, j)
         for j in range(4):
             EA(0, j, "S")
-        for j in range(4):
-            VM(0, j)
+        TV(0, 0)
+        TV(0, 1)
+        EV(0, 0, "V")
+        EV(0, 1, "S")
         QA(0, 0)
         QV(0)
         RT(0, 0, "V")
@@ -352,7 +362,10 @@ def tile_akgcn_pb_kernel(tc, x, hid, adj, lam_raw, theta, out):
             if u == 0:
                 A(1, 4)
                 Vs(1)
-                VR(1)
+                for j in range(4):
+                    V2(1, j)
+                for j in range(4):
+                    VD(1, j)
             if u == 1:
                 A(2, 4)
             if u == 2:
@@ -360,16 +373,15 @@ def tile_akgcn_pb_kernel(tc, x, hid, adj, lam_raw, theta, out):
             if u < 8:
                 M1(u, 0)
                 M1(u, 1)
-            if 0 <= z < 7:
-                ST(z, 0, 4)
-            if z == 7:
-                for j in range(4):
-                    ST(z, j, j + 1)
+            if 0 <= z < 8:
+                step = 4 // ST_PIECES[z]
+                for j in range(0, 4, step):
+                    ST(z, j, j + step)
             for k in range(4):
                 if u < 8:
                     if k >= 2:
                         M1(u, k)
-                    EH(u, k, "V" if k == 3 else "S")
+                    EH(u, k, "V" if (k == 3 and u != 0) else "S")
                 if 0 <= w < 8:
                     M2(w, k)
                     SG(w, k)
@@ -378,8 +390,8 @@ def tile_akgcn_pb_kernel(tc, x, hid, adj, lam_raw, theta, out):
             if 1 <= u <= 8:
                 RX(u - 1)
             if u == 1:
-                for j in range(4):
-                    VW(1, j)
-                for j in range(4):
-                    VM(1, j)
+                TV(1, 0)
+                TV(1, 1)
+                EV(1, 0, "S")
+                EV(1, 1, "V")
                 QV(1)

@@ -381,7 +381,7 @@ def tile_akgcn_pb_kernel(tc, x, hid, adj, lam_raw, theta, out):
                 if u < 8:
                     if k >= 2:
                         M1(u, k)
-                    EH(u, k, "V" if (k == 3 and u != 0) else "S")
+                    EH(u, k, "V" if (k == 3 and 1 <= u <= 6) else "S")
                 if 0 <= w < 8:
                     M2(w, k)
                     SG(w, k)

@@ -10,20 +10,16 @@ U8 = mybir.dt.uint8
 FP8X4 = mybir.dt.float8_e4m3fn_x4
 ALU = mybir.AluOpType
 ACT = mybir.ActivationFunctionType
-AX = mybir.AxisListType
 
 P = 128
 B, T, N, C = 2, 2, 512, 1024
 FLOPS = 2 * B * T * N * C * C + 2 * B * T * N * N * C
-PINNED = False
-ST_PIECES = (4, 4, 4, 4, 4, 4, 4, 4)
 
 
 def tile_akgcn_pb_kernel(tc, x, hid, adj, lam_raw, theta, out):
     nc = tc.nc
     with ExitStack() as ctx:
-        if PINNED:
-            ctx.enter_context(tc.manual_schedule())
+        ctx.enter_context(tc.manual_schedule())
         const = ctx.enter_context(tc.tile_pool(name="const", bufs=1))
         res = ctx.enter_context(tc.tile_pool(name="res", bufs=1))
         two = ctx.enter_context(tc.tile_pool(name="two", bufs=2))
@@ -40,17 +36,16 @@ def tile_akgcn_pb_kernel(tc, x, hid, adj, lam_raw, theta, out):
             else:
                 nc.scalar.copy(out=dst, in_=src)
 
+        lam_b = const.tile([P, 1], BF16)
+        nc.scalar.dma_start(out=lam_b[:], in_=lam_raw.partition_broadcast(P))
+
         ident_f = const.tile([P, P], F32)
         make_identity(nc, ident_f[:])
-        ident_b = const.tile([P, P], BF16)
-        make_identity(nc, ident_b[:])
         warm = const.tile([P, 1], F32)
         nc.vector.memset(warm[:], 0.0)
         warm2 = const.tile([P, 1], F32)
         nc.scalar.activation(out=warm2[:], in_=warm[:], func=ACT.Sigmoid)
 
-        lam_b = const.tile([P, 1], BF16)
-        nc.sync.dma_start(out=lam_b[:], in_=lam_raw.partition_broadcast(P))
 
         adj_sb = []
         for b in range(B):
@@ -69,16 +64,20 @@ def tile_akgcn_pb_kernel(tc, x, hid, adj, lam_raw, theta, out):
             th_raw.append(t_t)
 
         def load_adj(b):
-            nc.sync.dma_start(out=adj_sb[b][:], in_=adj[b].rearrange("(p j) m -> p (j m)", j=4))
+            for j in range(4):
+                nc.sync.dma_start(out=adj_sb[b][:, j * N : (j + 1) * N], in_=adj[b, j * P : (j + 1) * P])
 
         def load_hid(bt):
-            nc.sync.dma_start(
-                out=hid_sb[bt][:], in_=hid[bt // T, bt % T].rearrange("(p j) c -> p (j c)", j=4)
-            )
+            for u in range(2):
+                nc.sync.dma_start(
+                    out=hid_sb[bt][:, u * 2048 : (u + 1) * 2048],
+                    in_=hid[bt // T, bt % T, u * 256 : (u + 1) * 256].rearrange("(p e) c -> p (e c)", e=2),
+                )
 
         def load_x(bt):
             nc.sync.dma_start(
-                out=x_sb[bt][:], in_=x[bt // T, bt % T].rearrange("(p j) c -> p (j c)", j=4)
+                out=x_sb[bt][:].rearrange("p (j c) -> p j c", j=4),
+                in_=x[bt // T, bt % T].rearrange("(j p) c -> p j c", j=4),
             )
 
         def load_theta(ch):
@@ -91,15 +90,15 @@ def tile_akgcn_pb_kernel(tc, x, hid, adj, lam_raw, theta, out):
                 )
 
         load_adj(0)
-        load_adj(1)
         load_hid(0)
         load_theta(0)
         load_theta(1)
         load_hid(1)
-        load_hid(2)
         load_x(0)
-        load_hid(3)
+        load_adj(1)
+        load_hid(2)
         load_x(1)
+        load_hid(3)
         load_x(2)
         load_x(3)
 
@@ -117,72 +116,83 @@ def tile_akgcn_pb_kernel(tc, x, hid, adj, lam_raw, theta, out):
 
         st = {}
 
-        def V1(b, e):
-            rs = two.tile([P, 4], F32, name="rs")
-            st["rs", b] = rs
+        def V1(b, j, e="V"):
+            if j == 0:
+                rs = two.tile([P, 4], F32, name="rs")
+                st["rs", b] = rs
+            junk = four.tile([P, N], BF16, name="junk")
+            a_j = adj_sb[b][:, j * N : (j + 1) * N]
             if e == "V":
-                nc.vector.tensor_reduce(
-                    out=rs[:], in_=adj_sb[b][:].rearrange("p (j m) -> p j m", j=4), axis=AX.X, op=ALU.add
+                nc.vector.tensor_scalar(
+                    out=junk[:],
+                    in0=a_j,
+                    scalar1=1.0,
+                    scalar2=g32[:, 0:1],
+                    op0=ALU.mult,
+                    op1=ALU.add,
+                    accum_out=st["rs", b][:, j : j + 1],
                 )
             else:
-                for j in range(4):
-                    junk = const.tile([P, N], BF16, name="junk")
-                    nc.scalar.activation(
-                        out=junk[:],
-                        in_=adj_sb[b][:, j * N : (j + 1) * N],
-                        func=ACT.Copy,
-                        accum_out=rs[:, j : j + 1],
-                    )
+                rsa = two.tile([P, 1], F32, name="rsa")
+                nc.scalar.activation(out=junk[:], in_=a_j, func=ACT.Copy, accum_out=rsa[:])
+                st["rsa", b, j] = rsa
+
+        def V1g(b, j):
+            nc.vector.tensor_scalar(
+                out=st["rs", b][:, j : j + 1],
+                in0=st["rsa", b, j][:],
+                scalar1=g32[:, 0:1],
+                scalar2=None,
+                op0=ALU.add,
+            )
 
         def Vs(b):
-            den = two.tile([P, 4], F32, name="den")
-            nc.vector.tensor_scalar(
-                out=den[:], in0=st["rs", b][:], scalar1=g32[:, 0:1], scalar2=None, op0=ALU.add
-            )
             rec = two.tile([P, 4], F32, name="rec")
-            nc.vector.reciprocal(out=rec[:], in_=den[:])
-            grec = two.tile([P, 4], F32, name="grec")
-            nc.vector.tensor_scalar(
-                out=grec[:], in0=rec[:], scalar1=g32[:, 0:1], scalar2=None, op0=ALU.mult
-            )
+            nc.vector.reciprocal(out=rec[:], in_=st["rs", b][:])
             st["rec", b] = rec
-            st["grec", b] = grec
             vperm = const.tile([P, 4 * N], BF16, name="vperm")
             st["vperm", b] = vperm
 
         def V2(b, j):
-            src = adj_sb[b][:, j * N : (j + 1) * N].rearrange("q (p t) -> q t p", t=4)
             nc.vector.tensor_scalar(
-                out=st["vperm", b][:, j * N : (j + 1) * N].rearrange("q (t p) -> q t p", t=4),
-                in0=src,
+                out=st["vperm", b][:, j * N : (j + 1) * N],
+                in0=adj_sb[b][:, j * N : (j + 1) * N],
                 scalar1=st["rec", b][:, j : j + 1],
                 scalar2=None,
                 op0=ALU.mult,
             )
 
-        def VD(b, j):
-            src = adj_sb[b][:, j * N : (j + 1) * N].rearrange("q (p t) -> q t p", t=4)
-            dg = two.tile([P, P], F32, name="dg")
+        def DG(b, j):
+            dg = four.tile([P, P], F32, name="dg")
+            st["dg", b, j] = dg
             nc.vector.tensor_scalar(
-                out=dg[:], in0=ident_f[:], scalar1=st["grec", b][:, j : j + 1], scalar2=None, op0=ALU.mult
+                out=dg[:],
+                in0=ident_f[:],
+                scalar1=st["rec", b][:, j : j + 1],
+                scalar2=g32[:, 0:1],
+                op0=ALU.mult,
+                op1=ALU.mult,
             )
+
+        def VD(b, j):
             nc.vector.scalar_tensor_tensor(
                 out=st["vperm", b][:, j * N + j * P : j * N + (j + 1) * P],
-                in0=src[:, j, :],
+                in0=adj_sb[b][:, j * N + j * P : j * N + (j + 1) * P],
                 scalar=st["rec", b][:, j : j + 1],
-                in1=dg[:],
+                in1=st["dg", b, j][:],
                 op0=ALU.mult,
                 op1=ALU.add,
             )
 
         def TV(b, jp):
-            vt = ps.tile([P, 1024], BF16, tag="ps", name="vt")
+            vw = st["vperm", b][:].bitcast(F32)
+            vt = ps.tile([P, 512], F32, tag="ps", name="vt")
             st["vt", b, jp] = vt
-            for i in range(8):
+            for i in range(4):
                 nc.tensor.transpose(
                     vt[:, i * P : (i + 1) * P],
-                    st["vperm", b][:, (jp * 8 + i) * P : (jp * 8 + i + 1) * P],
-                    ident_b[:],
+                    vw[:, (jp * 4 + i) * P : (jp * 4 + i + 1) * P],
+                    ident_f[:],
                 )
 
         def EV(b, jp, e):
@@ -191,28 +201,32 @@ def tile_akgcn_pb_kernel(tc, x, hid, adj, lam_raw, theta, out):
                 st["vgrp", b] = vgrp
             copy(
                 e,
-                st["vgrp", b][:, jp * 1024 : (jp + 1) * 1024].rearrange("p (j n t) -> p j n t", j=2, t=4),
-                st["vt", b, jp][:].rearrange("p (j t n) -> p j n t", j=2, t=4),
+                st["vgrp", b][:].bitcast(F32)[:, jp * 512 : (jp + 1) * 512].rearrange("p (j n u) -> p j n u", j=2, u=2),
+                st["vt", b, jp][:].rearrange("p (j u n) -> p j n u", j=2, u=2),
             )
 
         def QV(b):
             nc.vector.quantize_mx(out=v_q[b][:].bitcast(FP8X4), scales=v_s[b][:], in_=st["vgrp", b][:])
 
-        def RT(ch, g, e):
-            if g == 0:
+        def RT(ch, g, e, c0, c1):
+            if ("tg", ch) not in st:
                 tg = two.tile([P, 4096], BF16, name="tg", align_bytes=64)
                 st["tg", ch] = tg
+            lo = g * 2048
             copy(
                 e,
-                st["tg", ch][:, g * 2048 : (g + 1) * 2048].rearrange("p (c i t) -> p c t i", i=4, t=4),
-                th_raw[ch][:, g * 2048 : (g + 1) * 2048].rearrange("p (t c i) -> p c t i", t=4, i=4),
+                st["tg", ch][:, lo + 4 * c0 : lo + 4 * c1].rearrange("p (c i t) -> p c t i", i=4, t=4),
+                th_raw[ch][:, lo : lo + 2048]
+                .rearrange("p (t c) -> p t c", t=4)[:, :, c0:c1]
+                .rearrange("p t (c i) -> p c t i", i=4),
             )
 
-        def QT(ch):
+        def QT(ch, g):
+            lo = ch * 1024 + g * 512
             nc.vector.quantize_mx(
-                out=th_q[:, ch * 1024 : (ch + 1) * 1024].bitcast(FP8X4),
-                scales=th_s[:, ch * 1024 : (ch + 1) * 1024],
-                in_=st["tg", ch][:],
+                out=th_q[:, lo : lo + 512].bitcast(FP8X4),
+                scales=th_s[:, lo : lo + 512],
+                in_=st["tg", ch][:, g * 2048 : (g + 1) * 2048],
             )
 
         def TA(bt, j):
@@ -248,14 +262,6 @@ def tile_akgcn_pb_kernel(tc, x, hid, adj, lam_raw, theta, out):
                 scales=hs[:, h * 512 : (h + 1) * 512],
                 in_=st["hg", bt][:, h * 2048 : (h + 1) * 2048],
             )
-
-        def A(bt, n_scalar):
-            for j in range(4):
-                TA(bt, j)
-            for j in range(4):
-                EA(bt, j, "S" if j < n_scalar else "V")
-                if j % 2 == 1:
-                    QA(bt, j // 2)
 
         def M1(u, k):
             bt, ch = u // 2, u % 2
@@ -328,70 +334,84 @@ def tile_akgcn_pb_kernel(tc, x, hid, adj, lam_raw, theta, out):
             nc.vector.scalar_tensor_tensor(
                 out=o3, in0=o3, scalar=0.5, in1=xview(u)[:, j0:j1, :], op0=ALU.max, op1=ALU.add
             )
-            o_v = out[bt // T, bt % T].rearrange("(p j) c -> p j c", j=4)
+            o_v = out[bt // T, bt % T].rearrange("(j p) c -> p j c", j=4)
             nc.sync.dma_start(out=o_v[:, j0:j1, ch * 512 : (ch + 1) * 512], in_=o3)
 
-        V1(0, "V")
-        V1(1, "S")
         nc.vector.tensor_scalar_max(out=g32[:], in0=lam_b[:], scalar1=0.0)
+        V1(0, 0)
+        V1(0, 2, "S")
+        V1(0, 3, "S")
+        V1(0, 1)
+        V1g(0, 2)
+        V1g(0, 3)
         Vs(0)
+        for j in range(4):
+            DG(0, j)
         for j in range(4):
             V2(0, j)
         for j in range(4):
             VD(0, j)
         for j in range(4):
             TA(0, j)
-        for j in range(4):
             EA(0, j, "S")
         TV(0, 0)
         TV(0, 1)
-        EV(0, 0, "V")
-        EV(0, 1, "S")
         QA(0, 0)
-        QV(0)
-        RT(0, 0, "V")
-        RT(0, 1, "S")
+        for g in range(2):
+            RT(0, g, "V", 0, 320)
+            RT(0, g, "S", 320, 512)
         QA(0, 1)
-        RT(1, 0, "V")
-        RT(1, 1, "S")
-        QT(0)
-        QT(1)
+        QT(0, 0)
+        QT(0, 1)
+        EV(0, 0, "S")
+        EV(0, 1, "S")
 
-        for u in range(11):
-            w, z = u - 2, u - 3
-            if u == 0:
-                A(1, 4)
-                Vs(1)
-                for j in range(4):
-                    V2(1, j)
-                for j in range(4):
-                    VD(1, j)
-            if u == 1:
-                A(2, 4)
-            if u == 2:
-                A(3, 3)
-            if u < 8:
-                M1(u, 0)
-                M1(u, 1)
-            if 0 <= z < 8:
-                step = 4 // ST_PIECES[z]
-                for j in range(0, 4, step):
-                    ST(z, j, j + step)
+        for u in range(9):
+            nbt, half = u // 2 + 1, u % 2
             for k in range(4):
                 if u < 8:
-                    if k >= 2:
-                        M1(u, k)
-                    EH(u, k, "V" if (k == 3 and 1 <= u <= 6) else "S")
-                if 0 <= w < 8:
-                    M2(w, k)
-                    SG(w, k)
-            if u < 8:
-                QH(u)
-            if 1 <= u <= 8:
-                RX(u - 1)
-            if u == 1:
-                TV(1, 0)
-                TV(1, 1)
-                EV(1, 0, "S")
-                EV(1, 1, "V")
-                QV(1)
+                    M1(u, k)
+                if nbt < 4 and k % 2 == 0:
+                    TA(nbt, 2 * half + k // 2)
+                if u < 8:
+                    EH(u, k, "V" if k == 1 and u > 2 else "S")
+                if nbt < 4 and k % 2 == 0:
+                    EA(nbt, 2 * half + k // 2, "S")
+                if u >= 1:
+                    if k == 0:
+                        QH(u - 1)
+                    for kk in ((), (0,), (1,), (2, 3))[k]:
+                        M2(u - 1, kk)
+                        SG(u - 1, kk)
+                if u >= 2 and k < 2:
+                    ST(u - 2, k + 2, k + 3)
+                if k == 1 and 1 <= u < 8:
+                    RX(u)
+                if k == 1 and u == 1:
+                    RX(0)
+                if u >= 1 and k >= 2:
+                    ST(u - 1, k - 2, k - 1)
+                if nbt < 4 and k == 3:
+                    QA(nbt, half)
+                if u == 0 and k == 0:
+                    RT(1, 0, "V", 0, 512)
+                    RT(1, 1, "V", 0, 512)
+                    QT(1, 0)
+                    QT(1, 1)
+                    QV(0)
+                if u == 1:
+                    V1(1, k)
+                if u == 2 and k == 0:
+                    Vs(1)
+                if u == 2:
+                    DG(1, k)
+                    V2(1, k)
+                if u == 3:
+                    VD(1, k)
+                if u == 4 and k < 2:
+                    TV(1, k)
+                    EV(1, k, "S")
+                if u == 4 and k == 3:
+                    QV(1)
+        ST(7, 2, 3)
+        ST(7, 3, 4)

@@ -36,11 +36,12 @@ def tile_akgcn_pb_kernel(tc, x, hid, adj, lam_raw, theta, out):
             else:
                 nc.scalar.copy(out=dst, in_=src)
 
-        lam_b = const.tile([P, 1], BF16)
-        nc.scalar.dma_start(out=lam_b[:], in_=lam_raw.partition_broadcast(P))
-
         ident_f = const.tile([P, P], F32)
         make_identity(nc, ident_f[:])
+        ones = const.tile([P, P], BF16)
+        nc.gpsimd.memset(ones[:], 1.0)
+        lam_b = const.tile([P, 1], BF16)
+        nc.gpsimd.memset(lam_b[:], 0.0)
         warm = const.tile([P, 1], F32)
         nc.vector.memset(warm[:], 0.0)
         warm2 = const.tile([P, 1], F32)
@@ -90,6 +91,7 @@ def tile_akgcn_pb_kernel(tc, x, hid, adj, lam_raw, theta, out):
                 )
 
         load_adj(0)
+        nc.sync.dma_start(out=lam_b[0:1, :], in_=lam_raw.unsqueeze(0))
         load_hid(0)
         load_theta(0)
         load_theta(1)
@@ -116,6 +118,11 @@ def tile_akgcn_pb_kernel(tc, x, hid, adj, lam_raw, theta, out):
 
         st = {}
 
+        def GL():
+            lam_p = ps.tile([P, 1], F32, tag="ps", name="lam_p")
+            nc.tensor.matmul(lam_p[:], lhsT=ones[:], rhs=lam_b[:], start=True, stop=True)
+            nc.vector.tensor_scalar_max(out=g32[:], in0=lam_p[:], scalar1=0.0)
+
         def V1(b, j, e="V"):
             if j == 0:
                 rs = two.tile([P, 4], F32, name="rs")
@@ -127,28 +134,23 @@ def tile_akgcn_pb_kernel(tc, x, hid, adj, lam_raw, theta, out):
                     out=junk[:],
                     in0=a_j,
                     scalar1=1.0,
-                    scalar2=g32[:, 0:1],
+                    scalar2=None,
                     op0=ALU.mult,
                     op1=ALU.add,
                     accum_out=st["rs", b][:, j : j + 1],
                 )
             else:
-                rsa = two.tile([P, 1], F32, name="rsa")
-                nc.scalar.activation(out=junk[:], in_=a_j, func=ACT.Copy, accum_out=rsa[:])
-                st["rsa", b, j] = rsa
-
-        def V1g(b, j):
-            nc.vector.tensor_scalar(
-                out=st["rs", b][:, j : j + 1],
-                in0=st["rsa", b, j][:],
-                scalar1=g32[:, 0:1],
-                scalar2=None,
-                op0=ALU.add,
-            )
+                nc.scalar.activation(
+                    out=junk[:], in_=a_j, func=ACT.Copy, accum_out=st["rs", b][:, j : j + 1]
+                )
 
         def Vs(b):
+            den = two.tile([P, 4], F32, name="den")
+            nc.vector.tensor_scalar(
+                out=den[:], in0=st["rs", b][:], scalar1=g32[:, 0:1], scalar2=None, op0=ALU.add
+            )
             rec = two.tile([P, 4], F32, name="rec")
-            nc.vector.reciprocal(out=rec[:], in_=st["rs", b][:])
+            nc.vector.reciprocal(out=rec[:], in_=den[:])
             st["rec", b] = rec
             vperm = const.tile([P, 4 * N], BF16, name="vperm")
             st["vperm", b] = vperm
@@ -165,7 +167,7 @@ def tile_akgcn_pb_kernel(tc, x, hid, adj, lam_raw, theta, out):
         def DG(b, j):
             dg = four.tile([P, P], F32, name="dg")
             st["dg", b, j] = dg
-            nc.vector.tensor_scalar(
+            nc.gpsimd.tensor_scalar(
                 out=dg[:],
                 in0=ident_f[:],
                 scalar1=st["rec", b][:, j : j + 1],
@@ -337,13 +339,11 @@ def tile_akgcn_pb_kernel(tc, x, hid, adj, lam_raw, theta, out):
             o_v = out[bt // T, bt % T].rearrange("(j p) c -> p j c", j=4)
             nc.sync.dma_start(out=o_v[:, j0:j1, ch * 512 : (ch + 1) * 512], in_=o3)
 
-        nc.vector.tensor_scalar_max(out=g32[:], in0=lam_b[:], scalar1=0.0)
         V1(0, 0)
         V1(0, 2, "S")
         V1(0, 3, "S")
         V1(0, 1)
-        V1g(0, 2)
-        V1g(0, 3)
+        GL()
         Vs(0)
         for j in range(4):
             DG(0, j)
@@ -371,28 +371,32 @@ def tile_akgcn_pb_kernel(tc, x, hid, adj, lam_raw, theta, out):
             for k in range(4):
                 if u < 8:
                     M1(u, k)
-                if nbt < 4 and k % 2 == 0:
-                    TA(nbt, 2 * half + k // 2)
+                if nbt < 4 and k < 2:
+                    TA(nbt, 2 * half + k)
                 if u < 8:
-                    EH(u, k, "V" if k == 1 and u > 2 else "S")
-                if nbt < 4 and k % 2 == 0:
-                    EA(nbt, 2 * half + k // 2, "S")
+                    EH(u, k, "V" if k == 2 and u > 2 else "S")
+                if nbt < 4 and k < 2:
+                    EA(nbt, 2 * half + k, "S")
                 if u >= 1:
                     if k == 0:
                         QH(u - 1)
                     for kk in ((), (0,), (1,), (2, 3))[k]:
                         M2(u - 1, kk)
                         SG(u - 1, kk)
-                if u >= 2 and k < 2:
-                    ST(u - 2, k + 2, k + 3)
+                if u >= 2 and k == 0:
+                    ST(u - 2, 2, 3)
+                    ST(u - 2, 3, 4)
                 if k == 1 and 1 <= u < 8:
                     RX(u)
                 if k == 1 and u == 1:
                     RX(0)
-                if u >= 1 and k >= 2:
-                    ST(u - 1, k - 2, k - 1)
-                if nbt < 4 and k == 3:
+                if nbt < 4 and k == 2:
                     QA(nbt, half)
+                if 1 <= u < 8 and k == 3:
+                    ST(u - 1, 0, 1)
+                    ST(u - 1, 1, 2)
+                if u == 8 and k >= 2:
+                    ST(u - 1, k - 2, k - 1)
                 if u == 0 and k == 0:
                     RT(1, 0, "V", 0, 512)
                     RT(1, 1, "V", 0, 512)

@@ -41,7 +41,7 @@ def tile_akgcn_pb_kernel(tc, x, hid, adj, lam_raw, theta, out):
         ones = const.tile([P, P], BF16)
         nc.gpsimd.memset(ones[:], 1.0)
         lam_b = const.tile([P, 1], BF16)
-        nc.gpsimd.memset(lam_b[:], 0.0)
+        nc.vector.memset(lam_b[:], 0.0)
         warm = const.tile([P, 1], F32)
         nc.vector.memset(warm[:], 0.0)
         warm2 = const.tile([P, 1], F32)
@@ -64,12 +64,15 @@ def tile_akgcn_pb_kernel(tc, x, hid, adj, lam_raw, theta, out):
             t_t = res.tile([P, 8 * 512], BF16, name="thraw%d" % ch)
             th_raw.append(t_t)
 
-        def load_adj(b):
-            for j in range(4):
-                nc.sync.dma_start(out=adj_sb[b][:, j * N : (j + 1) * N], in_=adj[b, j * P : (j + 1) * P])
+        def load_adj(b, us=range(2)):
+            for u in us:
+                nc.sync.dma_start(
+                    out=adj_sb[b][:, u * 2 * N : (u + 1) * 2 * N],
+                    in_=adj[b, u * 256 : (u + 1) * 256].rearrange("(p e) m -> p (e m)", e=2),
+                )
 
-        def load_hid(bt):
-            for u in range(2):
+        def load_hid(bt, us=range(2)):
+            for u in us:
                 nc.sync.dma_start(
                     out=hid_sb[bt][:, u * 2048 : (u + 1) * 2048],
                     in_=hid[bt // T, bt % T, u * 256 : (u + 1) * 256].rearrange("(p e) c -> p (e c)", e=2),
@@ -77,8 +80,8 @@ def tile_akgcn_pb_kernel(tc, x, hid, adj, lam_raw, theta, out):
 
         def load_x(bt):
             nc.sync.dma_start(
-                out=x_sb[bt][:].rearrange("p (j c) -> p j c", j=4),
-                in_=x[bt // T, bt % T].rearrange("(j p) c -> p j c", j=4),
+                out=x_sb[bt][:].rearrange("p (u f) -> p u f", u=2),
+                in_=x[bt // T, bt % T].rearrange("(u p e) c -> p u (e c)", u=2, e=2),
             )
 
         def load_theta(ch):
@@ -90,12 +93,14 @@ def tile_akgcn_pb_kernel(tc, x, hid, adj, lam_raw, theta, out):
                     ),
                 )
 
-        load_adj(0)
+        load_adj(0, range(1))
         nc.sync.dma_start(out=lam_b[0:1, :], in_=lam_raw.unsqueeze(0))
+        load_adj(0, range(1, 2))
         load_hid(0)
         load_theta(0)
+        load_hid(1, range(1))
         load_theta(1)
-        load_hid(1)
+        load_hid(1, range(1, 2))
         load_x(0)
         load_adj(1)
         load_hid(2)
@@ -122,6 +127,11 @@ def tile_akgcn_pb_kernel(tc, x, hid, adj, lam_raw, theta, out):
             lam_p = ps.tile([P, 1], F32, tag="ps", name="lam_p")
             nc.tensor.matmul(lam_p[:], lhsT=ones[:], rhs=lam_b[:], start=True, stop=True)
             nc.vector.tensor_scalar_max(out=g32[:], in0=lam_p[:], scalar1=0.0)
+
+        def WU(n):
+            wu = ps.tile([P, N], F32, tag="ps", name="wu")
+            for i in range(n):
+                nc.tensor.matmul(wu[:], lhsT=ones[:], rhs=adj_sb[0][:, i * N : (i + 1) * N], start=True, stop=True)
 
         def V1(b, j, e="V"):
             if j == 0:
@@ -164,26 +174,34 @@ def tile_akgcn_pb_kernel(tc, x, hid, adj, lam_raw, theta, out):
                 op0=ALU.mult,
             )
 
+        def diag(tile, j):
+            lo = j * N + (j // 2) * 256 + j % 2
+            return tile[:, lo : lo + 255 : 2]
+
+        g_ident = const.tile([P, P], F32)
+
+        def GI():
+            nc.gpsimd.tensor_scalar(
+                out=g_ident[:], in0=ident_f[:], scalar1=g32[:, 0:1], scalar2=1.0, op0=ALU.mult, op1=ALU.mult
+            )
+
         def DG(b, j):
             dg = four.tile([P, P], F32, name="dg")
             st["dg", b, j] = dg
-            nc.gpsimd.tensor_scalar(
+            nc.gpsimd.tensor_tensor(
                 out=dg[:],
-                in0=ident_f[:],
-                scalar1=st["rec", b][:, j : j + 1],
-                scalar2=g32[:, 0:1],
-                op0=ALU.mult,
-                op1=ALU.mult,
+                in0=diag(adj_sb[b], j),
+                in1=g_ident[:],
+                op=ALU.add,
             )
 
         def VD(b, j):
-            nc.vector.scalar_tensor_tensor(
-                out=st["vperm", b][:, j * N + j * P : j * N + (j + 1) * P],
-                in0=adj_sb[b][:, j * N + j * P : j * N + (j + 1) * P],
-                scalar=st["rec", b][:, j : j + 1],
-                in1=st["dg", b, j][:],
+            nc.vector.tensor_scalar(
+                out=diag(st["vperm", b], j),
+                in0=st["dg", b, j][:],
+                scalar1=st["rec", b][:, j : j + 1],
+                scalar2=None,
                 op0=ALU.mult,
-                op1=ALU.add,
             )
 
         def TV(b, jp):
@@ -336,17 +354,22 @@ def tile_akgcn_pb_kernel(tc, x, hid, adj, lam_raw, theta, out):
             nc.vector.scalar_tensor_tensor(
                 out=o3, in0=o3, scalar=0.5, in1=xview(u)[:, j0:j1, :], op0=ALU.max, op1=ALU.add
             )
-            o_v = out[bt // T, bt % T].rearrange("(j p) c -> p j c", j=4)
-            nc.sync.dma_start(out=o_v[:, j0:j1, ch * 512 : (ch + 1) * 512], in_=o3)
+            o_v = out[bt // T, bt % T].rearrange("(u p e) c -> p u e c", u=2, e=2)
+            for j in range(j0, j1):
+                nc.sync.dma_start(
+                    out=o_v[:, j // 2, j % 2, ch * 512 : (ch + 1) * 512],
+                    in_=st["ot", u][:, j * 512 : (j + 1) * 512],
+                )
 
         V1(0, 0)
         V1(0, 2, "S")
         V1(0, 3, "S")
         V1(0, 1)
         GL()
-        Vs(0)
+        GI()
         for j in range(4):
             DG(0, j)
+        Vs(0)
         for j in range(4):
             V2(0, j)
         for j in range(4):
@@ -356,11 +379,12 @@ def tile_akgcn_pb_kernel(tc, x, hid, adj, lam_raw, theta, out):
             EA(0, j, "S")
         TV(0, 0)
         TV(0, 1)
+        WU(4)
         QA(0, 0)
+        QA(0, 1)
         for g in range(2):
             RT(0, g, "V", 0, 320)
             RT(0, g, "S", 320, 512)
-        QA(0, 1)
         QT(0, 0)
         QT(0, 1)
         EV(0, 0, "S")
@@ -407,8 +431,9 @@ def tile_akgcn_pb_kernel(tc, x, hid, adj, lam_raw, theta, out):
                     V1(1, k)
                 if u == 2 and k == 0:
                     Vs(1)
-                if u == 2:
+                if u == 1:
                     DG(1, k)
+                if u == 2:
                     V2(1, k)
                 if u == 3:
                     VD(1, k)

from contextlib import ExitStack

import concourse.mybir as mybir
from concourse.masks import make_identity

F32 = mybir.dt.float32
BF16 = mybir.dt.bfloat16
U32 = mybir.dt.uint32
U8 = mybir.dt.uint8
FP8X4 = mybir.dt.float8_e4m3fn_x4
ALU = mybir.AluOpType
ACT = mybir.ActivationFunctionType

P = 128
B, T, N, C = 2, 2, 512, 1024
FLOPS = 2 * B * T * N * C * C + 2 * B * T * N * N * C


def tile_akgcn_pb_kernel(tc, x, hid, adj, lam_raw, theta, out):
    nc = tc.nc
    with ExitStack() as ctx:
        ctx.enter_context(tc.manual_schedule())
        const = ctx.enter_context(tc.tile_pool(name="const", bufs=1))
        res = ctx.enter_context(tc.tile_pool(name="res", bufs=1))
        two = ctx.enter_context(tc.tile_pool(name="two", bufs=2))
        three = ctx.enter_context(tc.tile_pool(name="three", bufs=3))
        four = ctx.enter_context(tc.tile_pool(name="four", bufs=4))
        ps = ctx.enter_context(tc.psum_pool(name="ps", bufs=8))

        def eng(e):
            return nc.vector if e == "V" else nc.scalar

        def copy(e, dst, src):
            if e == "V":
                nc.vector.tensor_copy(out=dst, in_=src)
            else:
                nc.scalar.copy(out=dst, in_=src)

        ident_f = const.tile([P, P], F32)
        make_identity(nc, ident_f[:])
        ones = const.tile([P, P], BF16)
        nc.gpsimd.memset(ones[:], 1.0)
        lam_b = const.tile([P, 1], BF16)
        nc.vector.memset(lam_b[:], 0.0)
        warm = const.tile([P, 1], F32)
        nc.vector.memset(warm[:], 0.0)
        warm2 = const.tile([P, 1], F32)
        nc.scalar.activation(out=warm2[:], in_=warm[:], func=ACT.Sigmoid)


        adj_sb = []
        for b in range(B):
            a_t = res.tile([P, 4 * N], BF16, name="adj%d" % b)
            adj_sb.append(a_t)
        hid_sb = []
        x_sb = []
        for bt in range(B * T):
            h_t = res.tile([P, 4 * C], BF16, name="hid%d" % bt)
            hid_sb.append(h_t)
            x_t = res.tile([P, 4 * C], BF16, name="x%d" % bt)
            x_sb.append(x_t)
        th_raw = []
        for ch in range(2):
            t_t = res.tile([P, 8 * 512], BF16, name="thraw%d" % ch)
            th_raw.append(t_t)

        def load_adj(b, us=range(2)):
            for u in us:
                nc.sync.dma_start(
                    out=adj_sb[b][:, u * 2 * N : (u + 1) * 2 * N],
                    in_=adj[b, u * 256 : (u + 1) * 256].rearrange("(p e) m -> p (e m)", e=2),
                )

        def load_hid(bt, us=range(2)):
            for u in us:
                nc.sync.dma_start(
                    out=hid_sb[bt][:, u * 2048 : (u + 1) * 2048],
                    in_=hid[bt // T, bt % T, u * 256 : (u + 1) * 256].rearrange("(p e) c -> p (e c)", e=2),
                )

        def load_x(bt):
            nc.sync.dma_start(
                out=x_sb[bt][:].rearrange("p (u f) -> p u f", u=2),
                in_=x[bt // T, bt % T].rearrange("(u p e) c -> p u (e c)", u=2, e=2),
            )

        def load_theta(ch):
            for a in range(4):
                nc.sync.dma_start(
                    out=th_raw[ch][:, a * 1024 : (a + 1) * 1024].rearrange("q (e c) -> q e c", e=2),
                    in_=theta[a * 256 : (a + 1) * 256, ch * 512 : (ch + 1) * 512].rearrange(
                        "(q e) c -> q e c", e=2
                    ),
                )

        load_adj(0, range(1))
        nc.sync.dma_start(out=lam_b[0:1, :], in_=lam_raw.unsqueeze(0))
        load_adj(0, range(1, 2))
        load_hid(0)
        load_theta(0)
        load_hid(1, range(1))
        load_theta(1)
        load_hid(1, range(1, 2))
        load_x(0)
        load_adj(1)
        load_hid(2)
        load_x(1)
        load_hid(3)
        load_x(2)
        load_x(3)

        g32 = const.tile([P, 1], F32)

        th_q = res.tile([P, 2048], U32, align_bytes=64)
        th_s = res.tile([P, 2048], U8, align_bytes=64)
        v_q = []
        v_s = []
        for b in range(B):
            q_t = res.tile([P, 512], U32, name="vq%d" % b, align_bytes=64)
            s_t = res.tile([P, 512], U8, name="vs%d" % b, align_bytes=64)
            v_q.append(q_t)
            v_s.append(s_t)

        st = {}

        def GL():
            lam_p = ps.tile([P, 1], F32, tag="ps", name="lam_p")
            nc.tensor.matmul(lam_p[:], lhsT=ones[:], rhs=lam_b[:], start=True, stop=True)
            nc.vector.tensor_scalar_max(out=g32[:], in0=lam_p[:], scalar1=0.0)

        def WU(n):
            wu = ps.tile([P, N], F32, tag="ps", name="wu")
            for i in range(n):
                nc.tensor.matmul(wu[:], lhsT=ones[:], rhs=adj_sb[0][:, i * N : (i + 1) * N], start=True, stop=True)

        def V1(b, j, e="V"):
            if j == 0:
                rs = two.tile([P, 4], F32, name="rs")
                st["rs", b] = rs
            junk = four.tile([P, N], BF16, name="junk")
            a_j = adj_sb[b][:, j * N : (j + 1) * N]
            if e == "V":
                nc.vector.tensor_scalar(
                    out=junk[:],
                    in0=a_j,
                    scalar1=1.0,
                    scalar2=None,
                    op0=ALU.mult,
                    op1=ALU.add,
                    accum_out=st["rs", b][:, j : j + 1],
                )
            else:
                nc.scalar.activation(
                    out=junk[:], in_=a_j, func=ACT.Copy, accum_out=st["rs", b][:, j : j + 1]
                )

        def Vs(b):
            den = two.tile([P, 4], F32, name="den")
            nc.vector.tensor_scalar(
                out=den[:], in0=st["rs", b][:], scalar1=g32[:, 0:1], scalar2=None, op0=ALU.add
            )
            rec = two.tile([P, 4], F32, name="rec")
            nc.vector.reciprocal(out=rec[:], in_=den[:])
            st["rec", b] = rec
            vperm = const.tile([P, 4 * N], BF16, name="vperm")
            st["vperm", b] = vperm

        def V2(b, j):
            nc.vector.tensor_scalar(
                out=st["vperm", b][:, j * N : (j + 1) * N],
                in0=adj_sb[b][:, j * N : (j + 1) * N],
                scalar1=st["rec", b][:, j : j + 1],
                scalar2=None,
                op0=ALU.mult,
            )

        def diag(tile, j):
            lo = j * N + (j // 2) * 256 + j % 2
            return tile[:, lo : lo + 255 : 2]

        g_ident = const.tile([P, P], F32)

        def GI():
            nc.gpsimd.tensor_scalar(
                out=g_ident[:], in0=ident_f[:], scalar1=g32[:, 0:1], scalar2=1.0, op0=ALU.mult, op1=ALU.mult
            )

        def DG(b, j):
            dg = four.tile([P, P], F32, name="dg")
            st["dg", b, j] = dg
            nc.gpsimd.tensor_tensor(
                out=dg[:],
                in0=diag(adj_sb[b], j),
                in1=g_ident[:],
                op=ALU.add,
            )

        def VD(b, j):
            nc.vector.tensor_scalar(
                out=diag(st["vperm", b], j),
                in0=st["dg", b, j][:],
                scalar1=st["rec", b][:, j : j + 1],
                scalar2=None,
                op0=ALU.mult,
            )

        def TV(b, jp):
            vw = st["vperm", b][:].bitcast(F32)
            vt = ps.tile([P, 512], F32, tag="ps", name="vt")
            st["vt", b, jp] = vt
            for i in range(4):
                nc.tensor.transpose(
                    vt[:, i * P : (i + 1) * P],
                    vw[:, (jp * 4 + i) * P : (jp * 4 + i + 1) * P],
                    ident_f[:],
                )

        def EV(b, jp, e):
            if jp == 0:
                vgrp = const.tile([P, 4 * N], BF16, name="vgrp", align_bytes=64)
                st["vgrp", b] = vgrp
            copy(
                e,
                st["vgrp", b][:].bitcast(F32)[:, jp * 512 : (jp + 1) * 512].rearrange("p (j n u) -> p j n u", j=2, u=2),
                st["vt", b, jp][:].rearrange("p (j u n) -> p j n u", j=2, u=2),
            )

        def QV(b):
            nc.vector.quantize_mx(out=v_q[b][:].bitcast(FP8X4), scales=v_s[b][:], in_=st["vgrp", b][:])

        def RT(ch, g, e, c0, c1):
            if ("tg", ch) not in st:
                tg = two.tile([P, 4096], BF16, name="tg", align_bytes=64)
                st["tg", ch] = tg
            lo = g * 2048
            copy(
                e,
                st["tg", ch][:, lo + 4 * c0 : lo + 4 * c1].rearrange("p (c i t) -> p c t i", i=4, t=4),
                th_raw[ch][:, lo : lo + 2048]
                .rearrange("p (t c) -> p t c", t=4)[:, :, c0:c1]
                .rearrange("p t (c i) -> p c t i", i=4),
            )

        def QT(ch, g):
            lo = ch * 1024 + g * 512
            nc.vector.quantize_mx(
                out=th_q[:, lo : lo + 512].bitcast(FP8X4),
                scales=th_s[:, lo : lo + 512],
                in_=st["tg", ch][:, g * 2048 : (g + 1) * 2048],
            )

        def TA(bt, j):
            hw = hid_sb[bt][:].bitcast(F32)
            xt = ps.tile([P, 512], F32, tag="ps", name="xt")
            st["xt", bt, j] = xt
            for a in range(4):
                nc.tensor.transpose(
                    xt[:, a * P : (a + 1) * P],
                    hw[:, j * 512 + a * P : j * 512 + (a + 1) * P],
                    ident_f[:],
                )

        def EA(bt, j, e):
            if j == 0:
                hg = two.tile([P, 4096], BF16, name="hg", align_bytes=64)
                st["hg", bt] = hg
            hgw = st["hg", bt][:].bitcast(F32)
            copy(
                e,
                hgw[:, j * 512 : (j + 1) * 512].rearrange("p (g r u) -> p g r u", g=2, u=2),
                st["xt", bt, j][:].rearrange("p (g u r) -> p g r u", g=2, u=2),
            )

        def QA(bt, h):
            if h == 0:
                hq = three.tile([P, 1024], U32, name="hq", align_bytes=64)
                hs = three.tile([P, 1024], U8, name="hs", align_bytes=64)
                st["hq", bt] = (hq, hs)
            hq, hs = st["hq", bt]
            nc.vector.quantize_mx(
                out=hq[:, h * 512 : (h + 1) * 512].bitcast(FP8X4),
                scales=hs[:, h * 512 : (h + 1) * 512],
                in_=st["hg", bt][:, h * 2048 : (h + 1) * 2048],
            )

        def M1(u, k):
            bt, ch = u // 2, u % 2
            hq, hs = st["hq", bt]
            hp = ps.tile([P, 512], F32, tag="ps", name="hp")
            st["hp", u, k] = hp
            for j in range(4):
                for g in range(2):
                    lo = (j * 2 + g) * P
                    ro = ch * 1024 + g * 512 + k * P
                    nc.tensor.matmul_mx(
                        out=hp[:, j * P : (j + 1) * P],
                        lhsT=hq[:, lo : lo + P].bitcast(FP8X4),
                        lhsT_scale=hs[:, lo : lo + P],
                        rhs=th_q[:, ro : ro + P].bitcast(FP8X4),
                        rhs_scale=th_s[:, ro : ro + P],
                        start=(g == 0),
                        stop=(g == 1),
                    )

        def EH(u, k, e):
            if k == 0:
                h2g = three.tile([P, 2048], BF16, name="h2g", align_bytes=64)
                st["h2g", u] = h2g
            copy(
                e,
                st["h2g", u][:, k * 512 : (k + 1) * 512].rearrange("p (c j) -> p c j", j=4),
                st["hp", u, k][:].rearrange("p (j c) -> p c j", j=4),
            )

        def QH(u):
            h2q = four.tile([P, 512], U32, name="h2q", align_bytes=64)
            h2s = four.tile([P, 512], U8, name="h2s", align_bytes=64)
            st["h2q", u] = (h2q, h2s)
            nc.vector.quantize_mx(out=h2q[:].bitcast(FP8X4), scales=h2s[:], in_=st["h2g", u][:])

        def xview(u):
            bt, ch = u // 2, u % 2
            return x_sb[bt][:].rearrange("p (j c) -> p j c", j=4)[:, :, ch * 512 : (ch + 1) * 512]

        def RX(u):
            nc.vector.tensor_scalar_max(out=xview(u), in0=xview(u), scalar1=0.0)

        def M2(u, jn):
            b = u // 4
            h2q, h2s = st["h2q", u]
            op = ps.tile([P, 512], F32, tag="ps", name="op")
            st["op", u, jn] = op
            nc.tensor.matmul_mx(
                out=op[:],
                lhsT=v_q[b][:, jn * P : (jn + 1) * P].bitcast(FP8X4),
                lhsT_scale=v_s[b][:, jn * P : (jn + 1) * P],
                rhs=h2q[:].bitcast(FP8X4),
                rhs_scale=h2s[:],
                start=True,
                stop=True,
            )

        def SG(u, jn):
            if jn == 0:
                ot = four.tile([P, 2048], F32, name="ot")
                st["ot", u] = ot
            nc.scalar.activation(
                out=st["ot", u][:, jn * 512 : (jn + 1) * 512], in_=st["op", u, jn][:], func=ACT.Sigmoid
            )

        def ST(u, j0, j1):
            bt, ch = u // 2, u % 2
            o3 = st["ot", u][:].rearrange("p (j c) -> p j c", j=4)[:, j0:j1, :]
            nc.vector.scalar_tensor_tensor(
                out=o3, in0=o3, scalar=0.5, in1=xview(u)[:, j0:j1, :], op0=ALU.max, op1=ALU.add
            )
            o_v = out[bt // T, bt % T].rearrange("(u p e) c -> p u e c", u=2, e=2)
            for j in range(j0, j1):
                nc.sync.dma_start(
                    out=o_v[:, j // 2, j % 2, ch * 512 : (ch + 1) * 512],
                    in_=st["ot", u][:, j * 512 : (j + 1) * 512],
                )

        V1(0, 0)
        V1(0, 2, "S")
        V1(0, 3, "S")
        V1(0, 1)
        GL()
        GI()
        for j in range(4):
            DG(0, j)
        Vs(0)
        for j in range(4):
            V2(0, j)
        for j in range(4):
            VD(0, j)
        for j in range(4):
            TA(0, j)
            EA(0, j, "S")
        TV(0, 0)
        TV(0, 1)
        WU(4)
        QA(0, 0)
        QA(0, 1)
        for g in range(2):
            RT(0, g, "V", 0, 320)
            RT(0, g, "S", 320, 512)
        QT(0, 0)
        QT(0, 1)
        EV(0, 0, "S")
        EV(0, 1, "S")

        for u in range(9):
            nbt, half = u // 2 + 1, u % 2
            for k in range(4):
                if u < 8:
                    M1(u, k)
                if nbt < 4 and k < 2:
                    TA(nbt, 2 * half + k)
                if u < 8:
                    EH(u, k, "V" if k == 2 and u > 2 else "S")
                if nbt < 4 and k < 2:
                    EA(nbt, 2 * half + k, "S")
                if u >= 1:
                    if k == 0:
                        QH(u - 1)
                    for kk in ((), (0,), (1,), (2, 3))[k]:
                        M2(u - 1, kk)
                        SG(u - 1, kk)
                if u >= 2 and k == 0:
                    ST(u - 2, 2, 3)
                    ST(u - 2, 3, 4)
                if k == 1 and 1 <= u < 8:
                    RX(u)
                if k == 1 and u == 1:
                    RX(0)
                if nbt < 4 and k == 2:
                    QA(nbt, half)
                if 1 <= u < 8 and k == 3:
                    ST(u - 1, 0, 1)
                    ST(u - 1, 1, 2)
                if u == 8 and k >= 2:
                    ST(u - 1, k - 2, k - 1)
                if u == 0 and k == 0:
                    RT(1, 0, "V", 0, 512)
                    RT(1, 1, "V", 0, 512)
                    QT(1, 0)
                    QT(1, 1)
                    QV(0)
                if u == 1:
                    V1(1, k)
                if u == 2 and k == 0:
                    Vs(1)
                if u == 1:
                    DG(1, k)
                if u == 2:
                    V2(1, k)
                if u == 3:
                    VD(1, k)
                if u == 4 and k < 2:
                    TV(1, k)
                    EV(1, k, "S")
                if u == 4 and k == 3:
                    QV(1)
        ST(7, 2, 3)
        ST(7, 3, 4)
